import numpy as np
import ml_dtypes


def mxq(x, axis, fmt="e4m3"):
    dtype, down = {"e4m3": (ml_dtypes.float8_e4m3fn, 7), "e5m2": (ml_dtypes.float8_e5m2, 14)}[fmt]
    v = np.moveaxis(np.asarray(x, np.float32).astype(ml_dtypes.bfloat16).astype(np.float64), axis, -1)
    blocks = v.reshape(v.shape[:-1] + (-1, 32))
    amax = np.abs(blocks).max(-1, keepdims=True)
    byte = np.maximum(np.where(amax > 0, np.frexp(amax)[1] - 1 + 127, 0) - down, 1)
    scale = np.exp2(byte - 127.0)
    codes = (blocks / scale).astype(np.float32).astype(dtype).astype(np.float64)
    return np.moveaxis((codes * scale).reshape(v.shape), -1, axis)


WIDE = False


def mx_kscale(k):
    if not WIDE:
        return np.ones(k)
    levels = np.array([10, -10, 5, -5, 0])
    a = np.random.permutation(np.resize(levels, k // 512 * 4)).reshape(k // 512, 4)
    idx = np.arange(k)
    return np.exp2(a[idx // 512, idx % 128 // 32])


BF16 = ml_dtypes.bfloat16


def bf(x):
    return np.asarray(x, np.float32).astype(BF16)


def f64(x):
    return np.asarray(x).astype(np.float64)


E2M1 = np.array([0.0, 0.5, 1.0, 1.5, 2.0, 3.0, 4.0, 6.0, -0.0, -0.5, -1.0, -1.5, -2.0, -3.0, -4.0, -6.0])


def pack_weight(w, fmt):
    k, n = w.shape
    w = f64(bf(w)).reshape(k // 32, 32, n)
    amax = np.abs(w).max(1)
    if fmt == "e4m3":
        byte = np.frexp(amax)[1] - 1 + 127 - 7
    else:
        mant, ex = np.frexp(amax / 6.0)
        byte = np.where(mant > 0.5, ex, ex - 1) + 127
    byte = np.clip(np.where(amax > 0, byte, 1), 1, 254)
    scaled = (w * np.exp2(127.0 - byte)[:, None, :]).reshape(k, n).astype(np.float32)
    by_word = np.ascontiguousarray(scaled.reshape(k // 512, 128, 4, n).transpose(0, 1, 3, 2))
    if fmt == "e4m3":
        words = by_word.astype(ml_dtypes.float8_e4m3fn).view(np.uint8)
    else:
        c = by_word.astype(ml_dtypes.float4_e2m1fn).view(np.uint8) & 0xF
        words = c[..., 0::2] | (c[..., 1::2] << 4)
    return np.ascontiguousarray(words), np.ascontiguousarray(byte.astype(np.uint8).reshape(k // 512, 16, n))


def unpack_weight(words, scales, fmt):
    g, p, n, _ = words.shape
    if fmt == "e4m3":
        vals = np.ascontiguousarray(words).view(ml_dtypes.float8_e4m3fn).astype(np.float64)
    else:
        nib = np.empty((g, p, n, 4), np.uint8)
        nib[..., 0::2] = words & 0xF
        nib[..., 1::2] = words >> 4
        vals = E2M1[nib]
    vals = vals * np.repeat(np.exp2(scales.astype(np.float64) - 127.0), 8, axis=1)[..., None]
    return vals.transpose(0, 1, 3, 2).reshape(g * 512, n)


B, S, FIN, D, AF, F, H = 2, 64, 128, 1024, 2048, 16384, 16
EPS = 1e-3
FMT = "e4m3"


def layer_norm(v, gamma, beta):
    mu = v.mean(-1, keepdims=True)
    var = v.var(-1, keepdims=True)
    return (v - mu) / np.sqrt(var + EPS) * gamma + beta


def setup_inputs():
    r = np.random.standard_normal
    t = mx_kscale(F)
    h_attn = bf(r((B, S, D)))
    W1_words, W1_scales = pack_weight(r((D, F)) / np.sqrt(D) * t, FMT)
    b1 = bf(0.1 * r(F) * t)
    W2_words, W2_scales = pack_weight(r((F, D)) / np.sqrt(F) / t[:, None], FMT)
    b2 = bf(0.1 * r(D))
    g2 = bf(1.0 + 0.1 * r(D))
    beta2 = bf(0.1 * r(D))
    return {"h_attn": h_attn,
            "W1_words": W1_words, "W1_scales": W1_scales, "b1": b1,
            "W2_words": W2_words, "W2_scales": W2_scales, "b2": b2,
            "g2": g2, "beta2": beta2}


def reference(h_attn, W1_words, W1_scales, b1, W2_words, W2_scales, b2, g2, beta2):
    h = f64(h_attn)
    hid = np.maximum((mxq(h, 2, "e4m3") @ unpack_weight(W1_words, W1_scales, FMT)) + f64(b1), 0.0)
    ffn = (mxq(hid, 2, "e4m3") @ unpack_weight(W2_words, W2_scales, FMT)) + f64(b2)
    return layer_norm(h + ffn, f64(g2), f64(beta2))

@@ -1,0 +1,324 @@
+import concourse.mybir as mybir
+from concourse.masks import make_identity
+
+F32 = mybir.dt.float32
+BF16 = mybir.dt.bfloat16
+I32 = mybir.dt.int32
+U32 = mybir.dt.uint32
+U8 = mybir.dt.uint8
+FP8X4 = mybir.dt.float8_e4m3fn_x4
+ALU = mybir.AluOpType
+ACT = mybir.ActivationFunctionType
+
+P = 128
+PACK = 4
+GROUP = P * PACK
+BANK = 512
+D = 1024
+F = 16384
+EPS = 1e-3
+D_GROUPS = D // GROUP
+F_GROUPS = F // GROUP
+D_BANKS = D // BANK
+QUADS = 4
+SHARED = 4
+
+CHUNK_GROUPS = 4
+CHUNK_WORDS = CHUNK_GROUPS * D
+CHUNKS = F_GROUPS // CHUNK_GROUPS
+CHUNK_BUFS = 7
+ROUND = 2
+ROUNDS = F_GROUPS // ROUND
+ROUNDS_IN_CHUNK = CHUNK_GROUPS // ROUND
+
+FLOPS = 2 * P * D * F * 2
+
+
+def tile_ffnn_encoder_pc_k_kernel(
+    tc, h_attn, W1_words, W1_scales, b1, W2_words, W2_scales, b2, g2, beta2, out
+):
+    nc = tc.nc
+    h_dram = h_attn.flatten_outer_dims()
+    out_dram = out.flatten_outer_dims()
+    w1_dram = W1_words.rearrange("g p n t -> g p (n t)").bitcast(I32)
+    w2_dram = W2_words.rearrange("g p n t -> g p (n t)").bitcast(I32)
+    s1_dram = W1_scales.bitcast(I32)
+    s2_dram = W2_scales.bitcast(I32)
+
+    with tc.manual_schedule(), tc.tile_pool(name="keep", bufs=1) as keep, tc.tile_pool(
+        name="chunks", bufs=CHUNK_BUFS
+    ) as chunks, tc.tile_pool(name="work", bufs=2) as work:
+        w1_planes = keep.tile([P, D_GROUPS, F // SHARED], U8, align_bytes=64)
+        w2_planes = keep.tile([P, F_GROUPS // SHARED, D], U8, align_bytes=64)
+        nc.vector.memset(w1_planes[:].bitcast(I32), 0)
+        nc.vector.memset(w2_planes[:].bitcast(I32), 0)
+
+        def load_w1_planes():
+            for g in range(D_GROUPS):
+                for q in range(QUADS):
+                    nc.sync.dma_start(
+                        out=w1_planes[32 * q : 32 * q + 16, g, :].bitcast(I32),
+                        in_=s1_dram[g, 4 * q : 4 * q + 4, :].rearrange(
+                            "r (o n) -> o r n", o=SHARED
+                        ),
+                    )
+
+        def load_w2_planes():
+            for c in range(F_GROUPS // SHARED):
+                for q in range(QUADS):
+                    nc.sync.dma_start(
+                        out=w2_planes[32 * q : 32 * q + 16, c, :].bitcast(I32),
+                        in_=s2_dram[SHARED * c : SHARED * (c + 1), 4 * q : 4 * q + 4, :],
+                    )
+
+        chunk_tiles = []
+
+        def load_chunk():
+            i = len(chunk_tiles)
+            if i == 2 * CHUNKS:
+                return
+            words = chunks.tile([P, CHUNK_WORDS], U32, name="words", align_bytes=64)
+            chunk_tiles.append(words)
+            if i < CHUNKS:
+                cols = slice(i * CHUNK_GROUPS * GROUP, (i + 1) * CHUNK_GROUPS * GROUP)
+                nc.sync.dma_start(
+                    out=words[:].bitcast(I32).rearrange("p (g n) -> p g n", g=D_GROUPS),
+                    in_=w1_dram[:, :, cols].rearrange("g p n -> p g n"),
+                )
+            else:
+                c = i - CHUNKS
+                nc.sync.dma_start(
+                    out=words[:].bitcast(I32).rearrange("p (g n) -> p g n", g=CHUNK_GROUPS),
+                    in_=w2_dram[CHUNK_GROUPS * c : CHUNK_GROUPS * (c + 1)].rearrange(
+                        "g p n -> p g n"
+                    ),
+                )
+            if i == 0:
+                load_w1_planes()
+            if i == CHUNKS - 1:
+                load_w2_planes()
+
+        for i in range(CHUNK_BUFS):
+            load_chunk()
+
+        h_sb = keep.tile([P, D], BF16, align_bytes=64)
+        nc.scalar.dma_start(out=h_sb[:], in_=h_dram)
+        eps = keep.tile([P, 1], F32)
+        nc.gpsimd.memset(eps[:], EPS)
+        warm = keep.tile([P, 1], F32)
+        nc.scalar.activation(out=warm[:], in_=eps[:], func=ACT.Sqrt)
+        ident = keep.tile([P, P], F32)
+        make_identity(nc, ident[:])
+        b1_rows = keep.tile([P, GROUP], BF16)
+        nc.gpsimd.memset(b1_rows[:], 0.0)
+        nc.scalar.dma_start(
+            out=b1_rows[0:F_GROUPS, :], in_=b1.rearrange("(g k) -> g k", k=GROUP)
+        )
+        vec_rows = keep.tile([P, 3, D], BF16)
+        nc.gpsimd.memset(vec_rows[:], 0.0)
+        ones = keep.tile([P, P], BF16)
+        nc.gpsimd.memset(ones[:], 1.0)
+        for i, vec in enumerate((b2, g2, beta2)):
+            nc.scalar.dma_start(out=vec_rows[0:1, i, :], in_=vec.rearrange("(o n) -> o n", o=1))
+
+        hid_words = keep.tile([P, F_GROUPS, P], U32, align_bytes=64)
+        hid_planes = keep.tile([P, F_GROUPS, P], U8, align_bytes=64)
+
+        with tc.psum_pool(name="sums", bufs=2 * ROUND) as sums, tc.psum_pool(
+            name="flipped", bufs=2 * ROUND
+        ) as flipped:
+            h_pairs = h_sb[:].bitcast(F32)
+            h_flip = flipped.tile([P, D_GROUPS * 2, P], F32, name="flip")
+            for g in range(D_GROUPS):
+                for u in range(2):
+                    nc.tensor.transpose(
+                        h_flip[:, 2 * g + u, :],
+                        h_pairs[:, 256 * g + u : 256 * (g + 1) : 2],
+                        ident[:],
+                    )
+            h_packed = keep.tile([P, D_GROUPS, P, PACK], BF16, align_bytes=64)
+            nc.vector.tensor_copy(
+                out=h_packed[:].bitcast(F32),
+                in_=h_flip[:].rearrange("p (g u) m -> p g m u", u=2),
+            )
+            h_words = keep.tile([P, D_GROUPS, P], U32, align_bytes=64)
+            h_planes = keep.tile([P, D_GROUPS, P], U8, align_bytes=64)
+            nc.vector.quantize_mx(
+                out=h_words[:].rearrange("p g m -> p (g m)").bitcast(FP8X4),
+                scales=h_planes[:].rearrange("p g m -> p (g m)"),
+                in_=h_packed[:].rearrange("p g m t -> p (g m t)"),
+            )
+
+            b1_sorted = keep.tile([P, PACK, P], F32)
+            nc.vector.tensor_copy(
+                out=b1_sorted[:], in_=b1_rows[:].rearrange("g (p t) -> g t p", t=PACK)
+            )
+            b1_flip = flipped.tile([P, PACK, P], F32, name="flip")
+            for t in range(PACK):
+                nc.tensor.transpose(b1_flip[:, t, :], b1_sorted[:, t, :], ident[:])
+            b1_t = keep.tile([P, F_GROUPS, PACK], F32)
+            nc.vector.tensor_copy(
+                out=b1_t[:], in_=b1_flip[:, :, 0:F_GROUPS].rearrange("p t g -> p g t")
+            )
+
+            sorted_sums = {}
+            biased = {}
+            rectified = {}
+
+            def project(r):
+                w1_words = chunk_tiles[r // ROUNDS_IN_CHUNK][:].rearrange(
+                    "p (g n) -> p g n", g=D_GROUPS
+                )
+                for j in range(ROUND):
+                    G = ROUND * r + j
+                    cols = slice((G % CHUNK_GROUPS) * BANK, (G % CHUNK_GROUPS + 1) * BANK)
+                    offset = PACK * (G // 8)
+                    plane_cols = slice((G % 8) * BANK, (G % 8 + 1) * BANK)
+                    acc = sums.tile([P, BANK], F32, name="acc")
+                    for g in range(D_GROUPS):
+                        nc.tensor.matmul_mx(
+                            out=acc[:],
+                            lhsT=h_words[:, g, :].bitcast(FP8X4),
+                            lhsT_scale=h_planes[:, g, :],
+                            rhs=w1_words[:, g, cols].bitcast(FP8X4),
+                            rhs_scale=w1_planes[offset:P, g, plane_cols],
+                            start=(g == 0),
+                            stop=(g == D_GROUPS - 1),
+                        )
+                    tidy = work.tile([P, PACK, P], F32, name="tidy", bufs=2 * ROUND)
+                    nc.scalar.copy(
+                        out=tidy[:], in_=acc[:].rearrange("m (p t) -> m t p", t=PACK)
+                    )
+                    sorted_sums[G] = tidy
+
+            def flip(r):
+                banks = []
+                for j in range(ROUND):
+                    G = ROUND * r + j
+                    bank = flipped.tile([P, PACK, P], F32, name="flip")
+                    for t in range(PACK):
+                        nc.tensor.transpose(bank[:, t, :], sorted_sums[G][:, t, :], ident[:])
+                    banks.append(bank)
+                biased[r] = work.tile([P, ROUND, P, PACK], BF16, name="biased")
+                for j in range(ROUND):
+                    G = ROUND * r + j
+                    nc.vector.tensor_tensor(
+                        out=biased[r][:, j, :, :],
+                        in0=banks[j][:].rearrange("p t m -> p m t"),
+                        in1=b1_t[:, G, :].unsqueeze(1).to_broadcast([P, P, PACK]),
+                        op=ALU.add,
+                    )
+
+            def rectify(r):
+                rectified[r] = work.tile(
+                    [P, ROUND * P * PACK], BF16, name="rectified", align_bytes=64
+                )
+                nc.vector.tensor_scalar_max(
+                    out=rectified[r][:],
+                    in0=biased[r][:].rearrange("p j m t -> p (j m t)"),
+                    scalar1=0.0,
+                )
+
+            def quantise(r):
+                groups = slice(ROUND * r, ROUND * (r + 1))
+                nc.vector.quantize_mx(
+                    out=hid_words[:, groups, :].rearrange("p g m -> p (g m)").bitcast(FP8X4),
+                    scales=hid_planes[:, groups, :].rearrange("p g m -> p (g m)"),
+                    in_=rectified[r][:],
+                )
+
+            for r in range(ROUNDS + 2):
+                if r < ROUNDS:
+                    project(r)
+                    if r % ROUNDS_IN_CHUNK == ROUNDS_IN_CHUNK - 1:
+                        load_chunk()
+                if 1 <= r <= ROUNDS:
+                    flip(r - 1)
+                if r >= 2:
+                    quantise(r - 2)
+                if 1 <= r <= ROUNDS:
+                    rectify(r - 1)
+
+        with tc.psum_pool(name="total", bufs=1, reuse_waits="tile") as total, tc.psum_pool(
+            name="spread", bufs=2, reuse_waits="tile"
+        ) as spread:
+            resid = keep.tile([P, D], F32)
+            gain = keep.tile([P, D], F32)
+            shift = keep.tile([P, D], F32)
+            for b in range(D_BANKS):
+                cols = slice(b * BANK, (b + 1) * BANK)
+                b2_all = spread.tile([P, BANK], F32, name="all")
+                nc.tensor.matmul(
+                    out=b2_all[:], lhsT=ones[:], rhs=vec_rows[:, 0, cols], start=True, stop=True
+                )
+                nc.vector.tensor_tensor(
+                    out=resid[:, cols], in0=b2_all[:], in1=h_sb[:, cols], op=ALU.add
+                )
+                g2_all = spread.tile([P, BANK], F32, name="all")
+                nc.tensor.matmul(
+                    out=g2_all[:], lhsT=ones[:], rhs=vec_rows[:, 1, cols], start=True, stop=True
+                )
+                nc.scalar.copy(out=gain[:, cols], in_=g2_all[:])
+                beta2_all = spread.tile([P, BANK], F32, name="all")
+                nc.tensor.matmul(
+                    out=beta2_all[:], lhsT=ones[:], rhs=vec_rows[:, 2, cols], start=True, stop=True
+                )
+                nc.scalar.copy(out=shift[:, cols], in_=beta2_all[:])
+
+            ffn = [total.tile([P, BANK], F32, name="ffn%d" % b) for b in range(D_BANKS)]
+            for c in range(CHUNKS):
+                w2_words = chunk_tiles[CHUNKS + c][:].rearrange(
+                    "p (g n) -> p g n", g=CHUNK_GROUPS
+                )
+                for j in range(CHUNK_GROUPS):
+                    G = CHUNK_GROUPS * c + j
+                    for b in range(D_BANKS):
+                        cols = slice(b * BANK, (b + 1) * BANK)
+                        nc.tensor.matmul_mx(
+                            out=ffn[b][:],
+                            lhsT=hid_words[:, G, :].bitcast(FP8X4),
+                            lhsT_scale=hid_planes[:, G, :],
+                            rhs=w2_words[:, j, cols].bitcast(FP8X4),
+                            rhs_scale=w2_planes[PACK * j : P, c, cols],
+                            start=(G == 0),
+                            stop=(G == F_GROUPS - 1),
+                        )
+                load_chunk()
+
+            r_sb = keep.tile([P, D], F32)
+            stats = keep.tile([P, D_BANKS, 6], F32)
+            for b in range(D_BANKS):
+                cols = slice(b * BANK, (b + 1) * BANK)
+                nc.vector.tensor_tensor(
+                    out=r_sb[:, cols], in0=ffn[b][:], in1=resid[:, cols], op=ALU.add
+                )
+            for b in range(D_BANKS):
+                cols = slice(b * BANK, (b + 1) * BANK)
+                nc.vector.bn_stats(out=stats[:, b, :], in_=r_sb[:, cols])
+            mean_var = keep.tile([P, 2], F32)
+            nc.vector.bn_aggr(out=mean_var[:], in_=stats[:].rearrange("p b s -> p (b s)"))
+            std = keep.tile([P, 1], F32)
+            nc.scalar.activation(out=std[:], in_=mean_var[:, 1:2], func=ACT.Sqrt, bias=eps[:])
+            centred = keep.tile([P, D], F32)
+            nc.vector.scalar_tensor_tensor(
+                out=centred[:],
+                in0=r_sb[:],
+                scalar=mean_var[:, 0:1],
+                in1=gain[:],
+                op0=ALU.subtract,
+                op1=ALU.mult,
+            )
+            inv_std = keep.tile([P, 1], F32)
+            nc.vector.reciprocal(out=inv_std[:], in_=std[:])
+            normed = keep.tile([P, D], F32)
+            for b in range(D_BANKS):
+                cols = slice(b * BANK, (b + 1) * BANK)
+                nc.vector.scalar_tensor_tensor(
+                    out=normed[:, cols],
+                    in0=centred[:, cols],
+                    scalar=inv_std[:],
+                    in1=shift[:, cols],
+                    op0=ALU.mult,
+                    op1=ALU.add,
+                )
+                nc.sync.dma_start(out=out_dram[:, cols], in_=normed[:, cols])

@@ -42,34 +42,36 @@ def tile_ffnn_encoder_pc_k_kernel(
     out_dram = out.flatten_outer_dims()
     w1_dram = W1_words.rearrange("g p n t -> g p (n t)").bitcast(I32)
     w2_dram = W2_words.rearrange("g p n t -> g p (n t)").bitcast(I32)
-    s1_dram = W1_scales.bitcast(I32)
-    s2_dram = W2_scales.bitcast(I32)
+    s1_dram = W1_scales.bitcast(F32)
+    s2_dram = W2_scales.bitcast(F32)
 
     with tc.manual_schedule(), tc.tile_pool(name="keep", bufs=1) as keep, tc.tile_pool(
         name="chunks", bufs=CHUNK_BUFS
     ) as chunks, tc.tile_pool(name="work", bufs=2) as work:
+        eps = keep.tile([P, 1], F32)
+        nc.gpsimd.memset(eps[:], EPS)
+        warm = keep.tile([P, 1], F32)
+        nc.scalar.activation(out=warm[:], in_=eps[:], func=ACT.Sqrt)
+        ident = keep.tile([P, P], F32)
+        make_identity(nc, ident[:])
+
         w1_planes = keep.tile([P, D_GROUPS, F // SHARED], U8, align_bytes=64)
         w2_planes = keep.tile([P, F_GROUPS // SHARED, D], U8, align_bytes=64)
         nc.vector.memset(w1_planes[:].bitcast(I32), 0)
         nc.vector.memset(w2_planes[:].bitcast(I32), 0)
-
-        def load_w1_planes():
-            for g in range(D_GROUPS):
-                for q in range(QUADS):
-                    nc.sync.dma_start(
-                        out=w1_planes[32 * q : 32 * q + 16, g, :].bitcast(I32),
-                        in_=s1_dram[g, 4 * q : 4 * q + 4, :].rearrange(
-                            "r (o n) -> o r n", o=SHARED
-                        ),
-                    )
-
-        def load_w2_planes():
-            for c in range(F_GROUPS // SHARED):
-                for q in range(QUADS):
-                    nc.sync.dma_start(
-                        out=w2_planes[32 * q : 32 * q + 16, c, :].bitcast(I32),
-                        in_=s2_dram[SHARED * c : SHARED * (c + 1), 4 * q : 4 * q + 4, :],
-                    )
+        for g in range(D_GROUPS):
+            for q in range(QUADS):
+                nc.gpsimd.dma_start(
+                    out=w1_planes[32 * q : 32 * q + 16, g, :].bitcast(F32),
+                    in_=s1_dram[g, 4 * q : 4 * q + 4, :].rearrange("r (o n) -> o r n", o=SHARED),
+                )
+        s2_rows = s2_dram.rearrange("(c o) s n -> s o c n", o=SHARED)
+        for q in range(QUADS):
+            for r in range(4):
+                nc.gpsimd.dma_start(
+                    out=w2_planes[32 * q + r : 32 * q + 16 : 4, :, :].bitcast(F32),
+                    in_=s2_rows[4 * q + r],
+                )
 
         chunk_tiles = []
 
@@ -93,31 +95,21 @@ def tile_ffnn_encoder_pc_k_kernel(
                         "g p n -> p g n"
                     ),
                 )
-            if i == 0:
-                load_w1_planes()
-            if i == CHUNKS - 1:
-                load_w2_planes()
 
         for i in range(CHUNK_BUFS):
             load_chunk()
 
         h_sb = keep.tile([P, D], BF16, align_bytes=64)
         nc.scalar.dma_start(out=h_sb[:], in_=h_dram)
-        eps = keep.tile([P, 1], F32)
-        nc.gpsimd.memset(eps[:], EPS)
-        warm = keep.tile([P, 1], F32)
-        nc.scalar.activation(out=warm[:], in_=eps[:], func=ACT.Sqrt)
-        ident = keep.tile([P, P], F32)
-        make_identity(nc, ident[:])
         b1_rows = keep.tile([P, GROUP], BF16)
-        nc.gpsimd.memset(b1_rows[:], 0.0)
+        nc.vector.memset(b1_rows[:], 0.0)
         nc.scalar.dma_start(
             out=b1_rows[0:F_GROUPS, :], in_=b1.rearrange("(g k) -> g k", k=GROUP)
         )
         vec_rows = keep.tile([P, 3, D], BF16)
-        nc.gpsimd.memset(vec_rows[:], 0.0)
+        nc.vector.memset(vec_rows[:], 0.0)
         ones = keep.tile([P, P], BF16)
-        nc.gpsimd.memset(ones[:], 1.0)
+        nc.vector.memset(ones[:], 1.0)
         for i, vec in enumerate((b2, g2, beta2)):
             nc.scalar.dma_start(out=vec_rows[0:1, i, :], in_=vec.rearrange("(o n) -> o n", o=1))
 

@@ -30,6 +30,7 @@ CHUNK_BUFS = 7
 ROUND = 2
 ROUNDS = F_GROUPS // ROUND
 ROUNDS_IN_CHUNK = CHUNK_GROUPS // ROUND
+STEP_BANKS = 3
 
 FLOPS = 2 * P * D * F * 2
 
@@ -47,7 +48,14 @@ def tile_ffnn_encoder_pc_k_kernel(
 
     with tc.manual_schedule(), tc.tile_pool(name="keep", bufs=1) as keep, tc.tile_pool(
         name="chunks", bufs=CHUNK_BUFS
-    ) as chunks, tc.tile_pool(name="work", bufs=2) as work:
+    ) as chunks, tc.tile_pool(name="work", bufs=2) as work, tc.psum_pool(
+        name="sums", bufs=STEP_BANKS
+    ) as sums, tc.psum_pool(name="flipped", bufs=STEP_BANKS) as flipped, tc.psum_pool(
+        name="total", bufs=1
+    ) as total:
+        h_sb = keep.tile([P, D], BF16, align_bytes=64)
+        nc.scalar.dma_start(out=h_sb[:], in_=h_dram)
+
         eps = keep.tile([P, 1], F32)
         nc.gpsimd.memset(eps[:], EPS)
         warm = keep.tile([P, 1], F32)
@@ -58,49 +66,55 @@ def tile_ffnn_encoder_pc_k_kernel(
         w1_planes = keep.tile([P, D_GROUPS, F // SHARED], U8, align_bytes=64)
         w2_planes = keep.tile([P, F_GROUPS // SHARED, D], U8, align_bytes=64)
         nc.vector.memset(w1_planes[:].bitcast(I32), 0)
-        nc.vector.memset(w2_planes[:].bitcast(I32), 0)
         for g in range(D_GROUPS):
             for q in range(QUADS):
                 nc.gpsimd.dma_start(
                     out=w1_planes[32 * q : 32 * q + 16, g, :].bitcast(F32),
                     in_=s1_dram[g, 4 * q : 4 * q + 4, :].rearrange("r (o n) -> o r n", o=SHARED),
                 )
-        s2_rows = s2_dram.rearrange("(c o) s n -> s o c n", o=SHARED)
-        for q in range(QUADS):
-            for r in range(4):
+        nc.vector.memset(w2_planes[:].bitcast(I32), 0)
+        for c in range(F_GROUPS // SHARED):
+            for q in range(QUADS):
                 nc.gpsimd.dma_start(
-                    out=w2_planes[32 * q + r : 32 * q + 16 : 4, :, :].bitcast(F32),
-                    in_=s2_rows[4 * q + r],
+                    out=w2_planes[32 * q : 32 * q + 16, c, :].bitcast(F32),
+                    in_=s2_dram[SHARED * c : SHARED * (c + 1), 4 * q : 4 * q + 4, :],
                 )
 
-        chunk_tiles = []
+        stream = []
+        for c in range(CHUNKS):
+            stream.append((1, c))
+            if c >= 1:
+                stream.append((2, c - 1))
+        stream.append((2, CHUNKS - 1))
+        w1_chunks = {}
+        w2_chunks = {}
 
         def load_chunk():
-            i = len(chunk_tiles)
-            if i == 2 * CHUNKS:
+            i = len(w1_chunks) + len(w2_chunks)
+            if i == len(stream):
                 return
+            weight, c = stream[i]
             words = chunks.tile([P, CHUNK_WORDS], U32, name="words", align_bytes=64)
-            chunk_tiles.append(words)
-            if i < CHUNKS:
-                cols = slice(i * CHUNK_GROUPS * GROUP, (i + 1) * CHUNK_GROUPS * GROUP)
+            if weight == 1:
+                w1_chunks[c] = words[:].rearrange("p (g n) -> p g n", g=D_GROUPS)
+                cols = slice(c * CHUNK_GROUPS * GROUP, (c + 1) * CHUNK_GROUPS * GROUP)
                 nc.sync.dma_start(
-                    out=words[:].bitcast(I32).rearrange("p (g n) -> p g n", g=D_GROUPS),
+                    out=w1_chunks[c].bitcast(I32),
                     in_=w1_dram[:, :, cols].rearrange("g p n -> p g n"),
                 )
             else:
-                c = i - CHUNKS
-                nc.sync.dma_start(
-                    out=words[:].bitcast(I32).rearrange("p (g n) -> p g n", g=CHUNK_GROUPS),
-                    in_=w2_dram[CHUNK_GROUPS * c : CHUNK_GROUPS * (c + 1)].rearrange(
-                        "g p n -> p g n"
-                    ),
-                )
+                w2_chunks[c] = words[:].rearrange("p (g n) -> p g n", g=CHUNK_GROUPS)
+                piece = 1 if c == CHUNKS - 1 else CHUNK_GROUPS
+                for j in range(0, CHUNK_GROUPS, piece):
+                    first = CHUNK_GROUPS * c + j
+                    nc.sync.dma_start(
+                        out=w2_chunks[c][:, j : j + piece, :].bitcast(I32),
+                        in_=w2_dram[first : first + piece].rearrange("g p n -> p g n"),
+                    )
 
         for i in range(CHUNK_BUFS):
             load_chunk()
 
-        h_sb = keep.tile([P, D], BF16, align_bytes=64)
-        nc.scalar.dma_start(out=h_sb[:], in_=h_dram)
         b1_rows = keep.tile([P, GROUP], BF16)
         nc.vector.memset(b1_rows[:], 0.0)
         nc.scalar.dma_start(
@@ -113,204 +127,185 @@ def tile_ffnn_encoder_pc_k_kernel(
         for i, vec in enumerate((b2, g2, beta2)):
             nc.scalar.dma_start(out=vec_rows[0:1, i, :], in_=vec.rearrange("(o n) -> o n", o=1))
 
+        h_pairs = h_sb[:].bitcast(F32)
+        h_flip = flipped.tile([P, D_GROUPS * 2, P], F32, name="flip")
+        for g in range(D_GROUPS):
+            for u in range(2):
+                nc.tensor.transpose(
+                    h_flip[:, 2 * g + u, :], h_pairs[:, 256 * g + u : 256 * (g + 1) : 2], ident[:]
+                )
+        h_packed = keep.tile([P, D_GROUPS, P, PACK], BF16, align_bytes=64)
+        nc.vector.tensor_copy(
+            out=h_packed[:].bitcast(F32), in_=h_flip[:].rearrange("p (g u) m -> p g m u", u=2)
+        )
+        h_words = keep.tile([P, D_GROUPS, P], U32, align_bytes=64)
+        h_planes = keep.tile([P, D_GROUPS, P], U8, align_bytes=64)
+        nc.vector.quantize_mx(
+            out=h_words[:].rearrange("p g m -> p (g m)").bitcast(FP8X4),
+            scales=h_planes[:].rearrange("p g m -> p (g m)"),
+            in_=h_packed[:].rearrange("p g m t -> p (g m t)"),
+        )
+
+        b1_sorted = keep.tile([P, PACK, P], F32)
+        nc.vector.tensor_copy(
+            out=b1_sorted[:], in_=b1_rows[:].rearrange("g (p t) -> g t p", t=PACK)
+        )
+        b1_flip = flipped.tile([P, PACK, P], F32, name="flip")
+        for t in range(PACK):
+            nc.tensor.transpose(b1_flip[:, t, :], b1_sorted[:, t, :], ident[:])
+        b1_t = keep.tile([P, F_GROUPS, PACK], F32)
+        nc.vector.tensor_copy(
+            out=b1_t[:], in_=b1_flip[:, :, 0:F_GROUPS].rearrange("p t g -> p g t")
+        )
+
+        resid = keep.tile([P, D], F32)
+        gain = keep.tile([P, D], F32)
+        shift = keep.tile([P, D], F32)
+        for b in range(D_BANKS):
+            cols = slice(b * BANK, (b + 1) * BANK)
+            b2_all = sums.tile([P, BANK], F32, name="acc")
+            nc.tensor.matmul(
+                out=b2_all[:], lhsT=ones[:], rhs=vec_rows[:, 0, cols], start=True, stop=True
+            )
+            nc.vector.tensor_tensor(
+                out=resid[:, cols], in0=b2_all[:], in1=h_sb[:, cols], op=ALU.add
+            )
+            g2_all = sums.tile([P, BANK], F32, name="acc")
+            nc.tensor.matmul(
+                out=g2_all[:], lhsT=ones[:], rhs=vec_rows[:, 1, cols], start=True, stop=True
+            )
+            nc.scalar.copy(out=gain[:, cols], in_=g2_all[:])
+            beta2_all = sums.tile([P, BANK], F32, name="acc")
+            nc.tensor.matmul(
+                out=beta2_all[:], lhsT=ones[:], rhs=vec_rows[:, 2, cols], start=True, stop=True
+            )
+            nc.scalar.copy(out=shift[:, cols], in_=beta2_all[:])
+
         hid_words = keep.tile([P, F_GROUPS, P], U32, align_bytes=64)
         hid_planes = keep.tile([P, F_GROUPS, P], U8, align_bytes=64)
+        ffn = [total.tile([P, BANK], F32, name="ffn%d" % b) for b in range(D_BANKS)]
+        sorted_sums = {}
+        biased = {}
+        rectified = {}
 
-        with tc.psum_pool(name="sums", bufs=2 * ROUND) as sums, tc.psum_pool(
-            name="flipped", bufs=2 * ROUND
-        ) as flipped:
-            h_pairs = h_sb[:].bitcast(F32)
-            h_flip = flipped.tile([P, D_GROUPS * 2, P], F32, name="flip")
-            for g in range(D_GROUPS):
-                for u in range(2):
-                    nc.tensor.transpose(
-                        h_flip[:, 2 * g + u, :],
-                        h_pairs[:, 256 * g + u : 256 * (g + 1) : 2],
-                        ident[:],
+        def project(r):
+            w1_words = w1_chunks[r // ROUNDS_IN_CHUNK]
+            for G in range(ROUND * r, ROUND * (r + 1)):
+                cols = slice((G % CHUNK_GROUPS) * BANK, (G % CHUNK_GROUPS + 1) * BANK)
+                offset = PACK * (G // 8)
+                plane_cols = slice((G % 8) * BANK, (G % 8 + 1) * BANK)
+                acc = sums.tile([P, BANK], F32, name="acc")
+                for g in range(D_GROUPS):
+                    nc.tensor.matmul_mx(
+                        out=acc[:],
+                        lhsT=h_words[:, g, :].bitcast(FP8X4),
+                        lhsT_scale=h_planes[:, g, :],
+                        rhs=w1_words[:, g, cols].bitcast(FP8X4),
+                        rhs_scale=w1_planes[offset:P, g, plane_cols],
+                        start=(g == 0),
+                        stop=(g == D_GROUPS - 1),
                     )
-            h_packed = keep.tile([P, D_GROUPS, P, PACK], BF16, align_bytes=64)
-            nc.vector.tensor_copy(
-                out=h_packed[:].bitcast(F32),
-                in_=h_flip[:].rearrange("p (g u) m -> p g m u", u=2),
+                tidy = work.tile([P, PACK, P], F32, name="tidy", bufs=2 * ROUND)
+                nc.scalar.copy(out=tidy[:], in_=acc[:].rearrange("m (p t) -> m t p", t=PACK))
+                sorted_sums[G] = tidy
+
+        def flip(r):
+            banks = {}
+            for G in range(ROUND * r, ROUND * (r + 1)):
+                banks[G] = flipped.tile([P, PACK, P], F32, name="flip")
+                for t in range(PACK):
+                    nc.tensor.transpose(banks[G][:, t, :], sorted_sums[G][:, t, :], ident[:])
+            biased[r] = work.tile([P, ROUND, P, PACK], BF16, name="biased")
+            for G in range(ROUND * r, ROUND * (r + 1)):
+                nc.vector.tensor_tensor(
+                    out=biased[r][:, G % ROUND, :, :],
+                    in0=banks[G][:].rearrange("p t m -> p m t"),
+                    in1=b1_t[:, G, :].unsqueeze(1).to_broadcast([P, P, PACK]),
+                    op=ALU.add,
+                )
+
+        def rectify(r):
+            rectified[r] = work.tile([P, ROUND * P * PACK], BF16, name="rectified", align_bytes=64)
+            nc.vector.tensor_scalar_max(
+                out=rectified[r][:],
+                in0=biased[r][:].rearrange("p j m t -> p (j m t)"),
+                scalar1=0.0,
             )
-            h_words = keep.tile([P, D_GROUPS, P], U32, align_bytes=64)
-            h_planes = keep.tile([P, D_GROUPS, P], U8, align_bytes=64)
+
+        def quantise(r):
+            groups = slice(ROUND * r, ROUND * (r + 1))
             nc.vector.quantize_mx(
-                out=h_words[:].rearrange("p g m -> p (g m)").bitcast(FP8X4),
-                scales=h_planes[:].rearrange("p g m -> p (g m)"),
-                in_=h_packed[:].rearrange("p g m t -> p (g m t)"),
+                out=hid_words[:, groups, :].rearrange("p g m -> p (g m)").bitcast(FP8X4),
+                scales=hid_planes[:, groups, :].rearrange("p g m -> p (g m)"),
+                in_=rectified[r][:],
             )
 
-            b1_sorted = keep.tile([P, PACK, P], F32)
-            nc.vector.tensor_copy(
-                out=b1_sorted[:], in_=b1_rows[:].rearrange("g (p t) -> g t p", t=PACK)
-            )
-            b1_flip = flipped.tile([P, PACK, P], F32, name="flip")
-            for t in range(PACK):
-                nc.tensor.transpose(b1_flip[:, t, :], b1_sorted[:, t, :], ident[:])
-            b1_t = keep.tile([P, F_GROUPS, PACK], F32)
-            nc.vector.tensor_copy(
-                out=b1_t[:], in_=b1_flip[:, :, 0:F_GROUPS].rearrange("p t g -> p g t")
-            )
-
-            sorted_sums = {}
-            biased = {}
-            rectified = {}
-
-            def project(r):
-                w1_words = chunk_tiles[r // ROUNDS_IN_CHUNK][:].rearrange(
-                    "p (g n) -> p g n", g=D_GROUPS
-                )
-                for j in range(ROUND):
-                    G = ROUND * r + j
-                    cols = slice((G % CHUNK_GROUPS) * BANK, (G % CHUNK_GROUPS + 1) * BANK)
-                    offset = PACK * (G // 8)
-                    plane_cols = slice((G % 8) * BANK, (G % 8 + 1) * BANK)
-                    acc = sums.tile([P, BANK], F32, name="acc")
-                    for g in range(D_GROUPS):
-                        nc.tensor.matmul_mx(
-                            out=acc[:],
-                            lhsT=h_words[:, g, :].bitcast(FP8X4),
-                            lhsT_scale=h_planes[:, g, :],
-                            rhs=w1_words[:, g, cols].bitcast(FP8X4),
-                            rhs_scale=w1_planes[offset:P, g, plane_cols],
-                            start=(g == 0),
-                            stop=(g == D_GROUPS - 1),
-                        )
-                    tidy = work.tile([P, PACK, P], F32, name="tidy", bufs=2 * ROUND)
-                    nc.scalar.copy(
-                        out=tidy[:], in_=acc[:].rearrange("m (p t) -> m t p", t=PACK)
-                    )
-                    sorted_sums[G] = tidy
-
-            def flip(r):
-                banks = []
-                for j in range(ROUND):
-                    G = ROUND * r + j
-                    bank = flipped.tile([P, PACK, P], F32, name="flip")
-                    for t in range(PACK):
-                        nc.tensor.transpose(bank[:, t, :], sorted_sums[G][:, t, :], ident[:])
-                    banks.append(bank)
-                biased[r] = work.tile([P, ROUND, P, PACK], BF16, name="biased")
-                for j in range(ROUND):
-                    G = ROUND * r + j
-                    nc.vector.tensor_tensor(
-                        out=biased[r][:, j, :, :],
-                        in0=banks[j][:].rearrange("p t m -> p m t"),
-                        in1=b1_t[:, G, :].unsqueeze(1).to_broadcast([P, P, PACK]),
-                        op=ALU.add,
+        def contract(r):
+            w2_words = w2_chunks[r // ROUNDS_IN_CHUNK]
+            for G in range(ROUND * r, ROUND * (r + 1)):
+                for b in range(D_BANKS):
+                    cols = slice(b * BANK, (b + 1) * BANK)
+                    nc.tensor.matmul_mx(
+                        out=ffn[b][:],
+                        lhsT=hid_words[:, G, :].bitcast(FP8X4),
+                        lhsT_scale=hid_planes[:, G, :],
+                        rhs=w2_words[:, G % CHUNK_GROUPS, cols].bitcast(FP8X4),
+                        rhs_scale=w2_planes[PACK * (G % SHARED) : P, G // SHARED, cols],
+                        start=(G == 0),
+                        stop=(G == F_GROUPS - 1),
                     )
 
-            def rectify(r):
-                rectified[r] = work.tile(
-                    [P, ROUND * P * PACK], BF16, name="rectified", align_bytes=64
-                )
-                nc.vector.tensor_scalar_max(
-                    out=rectified[r][:],
-                    in0=biased[r][:].rearrange("p j m t -> p (j m t)"),
-                    scalar1=0.0,
-                )
+        last_in_chunk = ROUNDS_IN_CHUNK - 1
+        for i in range(ROUNDS + 3):
+            if i < ROUNDS:
+                project(i)
+                if i % ROUNDS_IN_CHUNK == last_in_chunk:
+                    load_chunk()
+            if i >= 3:
+                contract(i - 3)
+                if (i - 3) % ROUNDS_IN_CHUNK == last_in_chunk:
+                    load_chunk()
+            if 1 <= i <= ROUNDS:
+                flip(i - 1)
+            if 2 <= i <= ROUNDS + 1:
+                quantise(i - 2)
+            if 1 <= i <= ROUNDS:
+                rectify(i - 1)
 
-            def quantise(r):
-                groups = slice(ROUND * r, ROUND * (r + 1))
-                nc.vector.quantize_mx(
-                    out=hid_words[:, groups, :].rearrange("p g m -> p (g m)").bitcast(FP8X4),
-                    scales=hid_planes[:, groups, :].rearrange("p g m -> p (g m)"),
-                    in_=rectified[r][:],
-                )
-
-            for r in range(ROUNDS + 2):
-                if r < ROUNDS:
-                    project(r)
-                    if r % ROUNDS_IN_CHUNK == ROUNDS_IN_CHUNK - 1:
-                        load_chunk()
-                if 1 <= r <= ROUNDS:
-                    flip(r - 1)
-                if r >= 2:
-                    quantise(r - 2)
-                if 1 <= r <= ROUNDS:
-                    rectify(r - 1)
-
-        with tc.psum_pool(name="total", bufs=1, reuse_waits="tile") as total, tc.psum_pool(
-            name="spread", bufs=2, reuse_waits="tile"
-        ) as spread:
-            resid = keep.tile([P, D], F32)
-            gain = keep.tile([P, D], F32)
-            shift = keep.tile([P, D], F32)
-            for b in range(D_BANKS):
-                cols = slice(b * BANK, (b + 1) * BANK)
-                b2_all = spread.tile([P, BANK], F32, name="all")
-                nc.tensor.matmul(
-                    out=b2_all[:], lhsT=ones[:], rhs=vec_rows[:, 0, cols], start=True, stop=True
-                )
-                nc.vector.tensor_tensor(
-                    out=resid[:, cols], in0=b2_all[:], in1=h_sb[:, cols], op=ALU.add
-                )
-                g2_all = spread.tile([P, BANK], F32, name="all")
-                nc.tensor.matmul(
-                    out=g2_all[:], lhsT=ones[:], rhs=vec_rows[:, 1, cols], start=True, stop=True
-                )
-                nc.scalar.copy(out=gain[:, cols], in_=g2_all[:])
-                beta2_all = spread.tile([P, BANK], F32, name="all")
-                nc.tensor.matmul(
-                    out=beta2_all[:], lhsT=ones[:], rhs=vec_rows[:, 2, cols], start=True, stop=True
-                )
-                nc.scalar.copy(out=shift[:, cols], in_=beta2_all[:])
-
-            ffn = [total.tile([P, BANK], F32, name="ffn%d" % b) for b in range(D_BANKS)]
-            for c in range(CHUNKS):
-                w2_words = chunk_tiles[CHUNKS + c][:].rearrange(
-                    "p (g n) -> p g n", g=CHUNK_GROUPS
-                )
-                for j in range(CHUNK_GROUPS):
-                    G = CHUNK_GROUPS * c + j
-                    for b in range(D_BANKS):
-                        cols = slice(b * BANK, (b + 1) * BANK)
-                        nc.tensor.matmul_mx(
-                            out=ffn[b][:],
-                            lhsT=hid_words[:, G, :].bitcast(FP8X4),
-                            lhsT_scale=hid_planes[:, G, :],
-                            rhs=w2_words[:, j, cols].bitcast(FP8X4),
-                            rhs_scale=w2_planes[PACK * j : P, c, cols],
-                            start=(G == 0),
-                            stop=(G == F_GROUPS - 1),
-                        )
-                load_chunk()
-
-            r_sb = keep.tile([P, D], F32)
-            stats = keep.tile([P, D_BANKS, 6], F32)
-            for b in range(D_BANKS):
-                cols = slice(b * BANK, (b + 1) * BANK)
-                nc.vector.tensor_tensor(
-                    out=r_sb[:, cols], in0=ffn[b][:], in1=resid[:, cols], op=ALU.add
-                )
-            for b in range(D_BANKS):
-                cols = slice(b * BANK, (b + 1) * BANK)
-                nc.vector.bn_stats(out=stats[:, b, :], in_=r_sb[:, cols])
-            mean_var = keep.tile([P, 2], F32)
-            nc.vector.bn_aggr(out=mean_var[:], in_=stats[:].rearrange("p b s -> p (b s)"))
-            std = keep.tile([P, 1], F32)
-            nc.scalar.activation(out=std[:], in_=mean_var[:, 1:2], func=ACT.Sqrt, bias=eps[:])
-            centred = keep.tile([P, D], F32)
+        r_sb = keep.tile([P, D], F32)
+        stats = keep.tile([P, D_BANKS, 6], F32)
+        for b in range(D_BANKS):
+            cols = slice(b * BANK, (b + 1) * BANK)
+            nc.vector.tensor_tensor(
+                out=r_sb[:, cols], in0=ffn[b][:], in1=resid[:, cols], op=ALU.add
+            )
+        for b in range(D_BANKS):
+            cols = slice(b * BANK, (b + 1) * BANK)
+            nc.vector.bn_stats(out=stats[:, b, :], in_=r_sb[:, cols])
+        mean_var = keep.tile([P, 2], F32)
+        nc.vector.bn_aggr(out=mean_var[:], in_=stats[:].rearrange("p b s -> p (b s)"))
+        std = keep.tile([P, 1], F32)
+        nc.scalar.activation(out=std[:], in_=mean_var[:, 1:2], func=ACT.Sqrt, bias=eps[:])
+        centred = keep.tile([P, D], F32)
+        nc.vector.scalar_tensor_tensor(
+            out=centred[:],
+            in0=r_sb[:],
+            scalar=mean_var[:, 0:1],
+            in1=gain[:],
+            op0=ALU.subtract,
+            op1=ALU.mult,
+        )
+        inv_std = keep.tile([P, 1], F32)
+        nc.vector.reciprocal(out=inv_std[:], in_=std[:])
+        normed = keep.tile([P, D], F32)
+        for b in range(D_BANKS):
+            cols = slice(b * BANK, (b + 1) * BANK)
             nc.vector.scalar_tensor_tensor(
-                out=centred[:],
-                in0=r_sb[:],
-                scalar=mean_var[:, 0:1],
-                in1=gain[:],
-                op0=ALU.subtract,
-                op1=ALU.mult,
+                out=normed[:, cols],
+                in0=centred[:, cols],
+                scalar=inv_std[:],
+                in1=shift[:, cols],
+                op0=ALU.mult,
+                op1=ALU.add,
             )
-            inv_std = keep.tile([P, 1], F32)
-            nc.vector.reciprocal(out=inv_std[:], in_=std[:])
-            normed = keep.tile([P, D], F32)
-            for b in range(D_BANKS):
-                cols = slice(b * BANK, (b + 1) * BANK)
-                nc.vector.scalar_tensor_tensor(
-                    out=normed[:, cols],
-                    in0=centred[:, cols],
-                    scalar=inv_std[:],
-                    in1=shift[:, cols],
-                    op0=ALU.mult,
-                    op1=ALU.add,
-                )
-                nc.sync.dma_start(out=out_dram[:, cols], in_=normed[:, cols])
+            nc.sync.dma_start(out=out_dram[:, cols], in_=normed[:, cols])

@@ -30,6 +30,8 @@ CHUNK_BUFS = 7
 ROUND = 2
 ROUNDS = F_GROUPS // ROUND
 ROUNDS_IN_CHUNK = CHUNK_GROUPS // ROUND
+LEAD = 2
+LAG = ROUNDS_IN_CHUNK * LEAD + 1
 STEP_BANKS = 3
 
 FLOPS = 2 * P * D * F * 2
@@ -81,11 +83,11 @@ def tile_ffnn_encoder_pc_k_kernel(
                 )
 
         stream = []
-        for c in range(CHUNKS):
-            stream.append((1, c))
-            if c >= 1:
-                stream.append((2, c - 1))
-        stream.append((2, CHUNKS - 1))
+        for c in range(CHUNKS + LEAD):
+            if c < CHUNKS:
+                stream.append((1, c))
+            if c >= LEAD:
+                stream.append((2, c - LEAD))
         w1_chunks = {}
         w2_chunks = {}
 
@@ -185,8 +187,6 @@ def tile_ffnn_encoder_pc_k_kernel(
         hid_planes = keep.tile([P, F_GROUPS, P], U8, align_bytes=64)
         ffn = [total.tile([P, BANK], F32, name="ffn%d" % b) for b in range(D_BANKS)]
         sorted_sums = {}
-        biased = {}
-        rectified = {}
 
         def project(r):
             w1_words = w1_chunks[r // ROUNDS_IN_CHUNK]
@@ -210,35 +210,33 @@ def tile_ffnn_encoder_pc_k_kernel(
                 sorted_sums[G] = tidy
 
         def flip(r):
+            groups = range(ROUND * r, ROUND * (r + 1))
             banks = {}
-            for G in range(ROUND * r, ROUND * (r + 1)):
+            for G in groups:
                 banks[G] = flipped.tile([P, PACK, P], F32, name="flip")
                 for t in range(PACK):
                     nc.tensor.transpose(banks[G][:, t, :], sorted_sums[G][:, t, :], ident[:])
-            biased[r] = work.tile([P, ROUND, P, PACK], BF16, name="biased")
-            for G in range(ROUND * r, ROUND * (r + 1)):
+            biased = work.tile([P, ROUND, P, PACK], BF16, name="biased")
+            rectified = work.tile([P, ROUND, P * PACK], BF16, name="rectified", align_bytes=64)
+            for G in groups:
                 nc.vector.tensor_tensor(
-                    out=biased[r][:, G % ROUND, :, :],
+                    out=biased[:, G % ROUND, :, :],
                     in0=banks[G][:].rearrange("p t m -> p m t"),
                     in1=b1_t[:, G, :].unsqueeze(1).to_broadcast([P, P, PACK]),
                     op=ALU.add,
                 )
-
-        def rectify(r):
-            rectified[r] = work.tile([P, ROUND * P * PACK], BF16, name="rectified", align_bytes=64)
-            nc.vector.tensor_scalar_max(
-                out=rectified[r][:],
-                in0=biased[r][:].rearrange("p j m t -> p (j m t)"),
-                scalar1=0.0,
-            )
-
-        def quantise(r):
-            groups = slice(ROUND * r, ROUND * (r + 1))
-            nc.vector.quantize_mx(
-                out=hid_words[:, groups, :].rearrange("p g m -> p (g m)").bitcast(FP8X4),
-                scales=hid_planes[:, groups, :].rearrange("p g m -> p (g m)"),
-                in_=rectified[r][:],
-            )
+            for G in groups:
+                nc.vector.tensor_scalar_max(
+                    out=rectified[:, G % ROUND, :],
+                    in0=biased[:, G % ROUND, :, :].rearrange("p m t -> p (m t)"),
+                    scalar1=0.0,
+                )
+            for G in groups:
+                nc.vector.quantize_mx(
+                    out=hid_words[:, G, :].bitcast(FP8X4),
+                    scales=hid_planes[:, G, :],
+                    in_=rectified[:, G % ROUND, :],
+                )
 
         def contract(r):
             w2_words = w2_chunks[r // ROUNDS_IN_CHUNK]
@@ -256,21 +254,17 @@ def tile_ffnn_encoder_pc_k_kernel(
                     )
 
         last_in_chunk = ROUNDS_IN_CHUNK - 1
-        for i in range(ROUNDS + 3):
+        for i in range(ROUNDS + LAG):
             if i < ROUNDS:
                 project(i)
                 if i % ROUNDS_IN_CHUNK == last_in_chunk:
                     load_chunk()
-            if i >= 3:
-                contract(i - 3)
-                if (i - 3) % ROUNDS_IN_CHUNK == last_in_chunk:
+            if i >= LAG:
+                contract(i - LAG)
+                if (i - LAG) % ROUNDS_IN_CHUNK == last_in_chunk:
                     load_chunk()
             if 1 <= i <= ROUNDS:
                 flip(i - 1)
-            if 2 <= i <= ROUNDS + 1:
-                quantise(i - 2)
-            if 1 <= i <= ROUNDS:
-                rectify(i - 1)
 
         r_sb = keep.tile([P, D], F32)
         stats = keep.tile([P, D_BANKS, 6], F32)

@@ -32,6 +32,7 @@ ROUNDS = F_GROUPS // ROUND
 ROUNDS_IN_CHUNK = CHUNK_GROUPS // ROUND
 LEAD = 2
 LAG = ROUNDS_IN_CHUNK * LEAD + 1
+SPREAD_STEP = 2
 STEP_BANKS = 3
 
 FLOPS = 2 * P * D * F * 2
@@ -68,13 +69,26 @@ def tile_ffnn_encoder_pc_k_kernel(
         w1_planes = keep.tile([P, D_GROUPS, F // SHARED], U8, align_bytes=64)
         w2_planes = keep.tile([P, F_GROUPS // SHARED, D], U8, align_bytes=64)
         nc.vector.memset(w1_planes[:].bitcast(I32), 0)
+        b1_rows = keep.tile([P, GROUP], BF16)
+        nc.vector.memset(b1_rows[:], 0.0)
+        vec_rows = keep.tile([P, 3, D], BF16)
+        nc.vector.memset(vec_rows[:], 0.0)
+        nc.vector.memset(w2_planes[:].bitcast(I32), 0)
+        ones = keep.tile([P, P], BF16)
+        nc.vector.memset(ones[:], 1.0)
+
+        nc.scalar.dma_start(
+            out=b1_rows[0:F_GROUPS, :], in_=b1.rearrange("(g k) -> g k", k=GROUP)
+        )
+        for i, vec in enumerate((b2, g2, beta2)):
+            nc.scalar.dma_start(out=vec_rows[0:1, i, :], in_=vec.rearrange("(o n) -> o n", o=1))
+
         for g in range(D_GROUPS):
             for q in range(QUADS):
                 nc.gpsimd.dma_start(
                     out=w1_planes[32 * q : 32 * q + 16, g, :].bitcast(F32),
                     in_=s1_dram[g, 4 * q : 4 * q + 4, :].rearrange("r (o n) -> o r n", o=SHARED),
                 )
-        nc.vector.memset(w2_planes[:].bitcast(I32), 0)
         for c in range(F_GROUPS // SHARED):
             for q in range(QUADS):
                 nc.gpsimd.dma_start(
@@ -117,18 +131,6 @@ def tile_ffnn_encoder_pc_k_kernel(
         for i in range(CHUNK_BUFS):
             load_chunk()
 
-        b1_rows = keep.tile([P, GROUP], BF16)
-        nc.vector.memset(b1_rows[:], 0.0)
-        nc.scalar.dma_start(
-            out=b1_rows[0:F_GROUPS, :], in_=b1.rearrange("(g k) -> g k", k=GROUP)
-        )
-        vec_rows = keep.tile([P, 3, D], BF16)
-        nc.vector.memset(vec_rows[:], 0.0)
-        ones = keep.tile([P, P], BF16)
-        nc.vector.memset(ones[:], 1.0)
-        for i, vec in enumerate((b2, g2, beta2)):
-            nc.scalar.dma_start(out=vec_rows[0:1, i, :], in_=vec.rearrange("(o n) -> o n", o=1))
-
         h_pairs = h_sb[:].bitcast(F32)
         h_flip = flipped.tile([P, D_GROUPS * 2, P], F32, name="flip")
         for g in range(D_GROUPS):
@@ -163,25 +165,26 @@ def tile_ffnn_encoder_pc_k_kernel(
         resid = keep.tile([P, D], F32)
         gain = keep.tile([P, D], F32)
         shift = keep.tile([P, D], F32)
-        for b in range(D_BANKS):
-            cols = slice(b * BANK, (b + 1) * BANK)
-            b2_all = sums.tile([P, BANK], F32, name="acc")
-            nc.tensor.matmul(
-                out=b2_all[:], lhsT=ones[:], rhs=vec_rows[:, 0, cols], start=True, stop=True
-            )
-            nc.vector.tensor_tensor(
-                out=resid[:, cols], in0=b2_all[:], in1=h_sb[:, cols], op=ALU.add
-            )
-            g2_all = sums.tile([P, BANK], F32, name="acc")
-            nc.tensor.matmul(
-                out=g2_all[:], lhsT=ones[:], rhs=vec_rows[:, 1, cols], start=True, stop=True
-            )
-            nc.scalar.copy(out=gain[:, cols], in_=g2_all[:])
-            beta2_all = sums.tile([P, BANK], F32, name="acc")
-            nc.tensor.matmul(
-                out=beta2_all[:], lhsT=ones[:], rhs=vec_rows[:, 2, cols], start=True, stop=True
-            )
-            nc.scalar.copy(out=shift[:, cols], in_=beta2_all[:])
+        def spread_vectors():
+            for b in range(D_BANKS):
+                cols = slice(b * BANK, (b + 1) * BANK)
+                b2_all = sums.tile([P, BANK], F32, name="acc")
+                nc.tensor.matmul(
+                    out=b2_all[:], lhsT=ones[:], rhs=vec_rows[:, 0, cols], start=True, stop=True
+                )
+                nc.vector.tensor_tensor(
+                    out=resid[:, cols], in0=b2_all[:], in1=h_sb[:, cols], op=ALU.add
+                )
+                g2_all = sums.tile([P, BANK], F32, name="acc")
+                nc.tensor.matmul(
+                    out=g2_all[:], lhsT=ones[:], rhs=vec_rows[:, 1, cols], start=True, stop=True
+                )
+                nc.scalar.copy(out=gain[:, cols], in_=g2_all[:])
+                beta2_all = sums.tile([P, BANK], F32, name="acc")
+                nc.tensor.matmul(
+                    out=beta2_all[:], lhsT=ones[:], rhs=vec_rows[:, 2, cols], start=True, stop=True
+                )
+                nc.scalar.copy(out=shift[:, cols], in_=beta2_all[:])
 
         hid_words = keep.tile([P, F_GROUPS, P], U32, align_bytes=64)
         hid_planes = keep.tile([P, F_GROUPS, P], U8, align_bytes=64)
@@ -265,6 +268,8 @@ def tile_ffnn_encoder_pc_k_kernel(
                     load_chunk()
             if 1 <= i <= ROUNDS:
                 flip(i - 1)
+            if i == SPREAD_STEP:
+                spread_vectors()
 
         r_sb = keep.tile([P, D], F32)
         stats = keep.tile([P, D_BANKS, 6], F32)

@@ -120,12 +120,14 @@ def tile_ffnn_encoder_pc_k_kernel(
                 )
             else:
                 w2_chunks[c] = words[:].rearrange("p (g n) -> p g n", g=CHUNK_GROUPS)
-                piece = 1 if c == CHUNKS - 1 else CHUNK_GROUPS
-                for j in range(0, CHUNK_GROUPS, piece):
-                    first = CHUNK_GROUPS * c + j
+                pieces = [(0, CHUNK_GROUPS, 0, D)]
+                if c == CHUNKS - 1:
+                    pieces = [(0, CHUNK_GROUPS, 0, BANK), (0, ROUND, BANK, D), (ROUND, CHUNK_GROUPS, BANK, D)]
+                for j0, j1, n0, n1 in pieces:
+                    groups = slice(CHUNK_GROUPS * c + j0, CHUNK_GROUPS * c + j1)
                     nc.sync.dma_start(
-                        out=w2_chunks[c][:, j : j + piece, :].bitcast(I32),
-                        in_=w2_dram[first : first + piece].rearrange("g p n -> p g n"),
+                        out=w2_chunks[c][:, j0:j1, n0:n1].bitcast(I32),
+                        in_=w2_dram[groups, :, n0:n1].rearrange("g p n -> p g n"),
                     )
 
         for i in range(CHUNK_BUFS):
@@ -241,23 +243,25 @@ def tile_ffnn_encoder_pc_k_kernel(
                     in_=rectified[:, G % ROUND, :],
                 )
 
+        def contract_bank(G, b):
+            cols = slice(b * BANK, (b + 1) * BANK)
+            nc.tensor.matmul_mx(
+                out=ffn[b][:],
+                lhsT=hid_words[:, G, :].bitcast(FP8X4),
+                lhsT_scale=hid_planes[:, G, :],
+                rhs=w2_chunks[G // CHUNK_GROUPS][:, G % CHUNK_GROUPS, cols].bitcast(FP8X4),
+                rhs_scale=w2_planes[PACK * (G % SHARED) : P, G // SHARED, cols],
+                start=(G == 0),
+                stop=(G == F_GROUPS - 1),
+            )
+
         def contract(r):
-            w2_words = w2_chunks[r // ROUNDS_IN_CHUNK]
             for G in range(ROUND * r, ROUND * (r + 1)):
                 for b in range(D_BANKS):
-                    cols = slice(b * BANK, (b + 1) * BANK)
-                    nc.tensor.matmul_mx(
-                        out=ffn[b][:],
-                        lhsT=hid_words[:, G, :].bitcast(FP8X4),
-                        lhsT_scale=hid_planes[:, G, :],
-                        rhs=w2_words[:, G % CHUNK_GROUPS, cols].bitcast(FP8X4),
-                        rhs_scale=w2_planes[PACK * (G % SHARED) : P, G // SHARED, cols],
-                        start=(G == 0),
-                        stop=(G == F_GROUPS - 1),
-                    )
+                    contract_bank(G, b)
 
         last_in_chunk = ROUNDS_IN_CHUNK - 1
-        for i in range(ROUNDS + LAG):
+        for i in range(ROUNDS + LAG - ROUNDS_IN_CHUNK):
             if i < ROUNDS:
                 project(i)
                 if i % ROUNDS_IN_CHUNK == last_in_chunk:
@@ -275,11 +279,11 @@ def tile_ffnn_encoder_pc_k_kernel(
         stats = keep.tile([P, D_BANKS, 6], F32)
         for b in range(D_BANKS):
             cols = slice(b * BANK, (b + 1) * BANK)
+            for G in range(F_GROUPS - CHUNK_GROUPS, F_GROUPS):
+                contract_bank(G, b)
             nc.vector.tensor_tensor(
                 out=r_sb[:, cols], in0=ffn[b][:], in1=resid[:, cols], op=ALU.add
             )
-        for b in range(D_BANKS):
-            cols = slice(b * BANK, (b + 1) * BANK)
             nc.vector.bn_stats(out=stats[:, b, :], in_=r_sb[:, cols])
         mean_var = keep.tile([P, 2], F32)
         nc.vector.bn_aggr(out=mean_var[:], in_=stats[:].rearrange("p b s -> p (b s)"))

@@ -26,7 +26,8 @@ SHARED = 4
 CHUNK_GROUPS = 4
 CHUNK_WORDS = CHUNK_GROUPS * D
 CHUNKS = F_GROUPS // CHUNK_GROUPS
-CHUNK_BUFS = 7
+PAIRS = CHUNKS // 2
+CHUNK_BUFS = 9
 ROUND = 2
 ROUNDS = F_GROUPS // ROUND
 ROUNDS_IN_CHUNK = CHUNK_GROUPS // ROUND
@@ -89,6 +90,7 @@ def tile_ffnn_encoder_pc_k_kernel(
                     out=w1_planes[32 * q : 32 * q + 16, g, :].bitcast(F32),
                     in_=s1_dram[g, 4 * q : 4 * q + 4, :].rearrange("r (o n) -> o r n", o=SHARED),
                 )
+
         for c in range(F_GROUPS // SHARED):
             for q in range(QUADS):
                 nc.gpsimd.dma_start(
@@ -97,27 +99,39 @@ def tile_ffnn_encoder_pc_k_kernel(
                 )
 
         stream = []
-        for c in range(CHUNKS + LEAD):
-            if c < CHUNKS:
-                stream.append((1, c))
-            if c >= LEAD:
-                stream.append((2, c - LEAD))
-        w1_chunks = {}
+        for pair in range(PAIRS + 1):
+            if pair == 0:
+                stream += [(1, 0, None), (1, 1, None)]
+            elif pair < PAIRS:
+                stream += [(1, pair, g) for g in range(D_GROUPS)]
+            if pair >= 1:
+                stream += [(2, 2 * pair - 2, None), (2, 2 * pair - 1, None)]
+        w1_groups = {}
         w2_chunks = {}
+        loads = []
 
         def load_chunk():
-            i = len(w1_chunks) + len(w2_chunks)
+            i = len(loads)
             if i == len(stream):
                 return
-            weight, c = stream[i]
+            weight, c, g = stream[i]
             words = chunks.tile([P, CHUNK_WORDS], U32, name="words", align_bytes=64)
-            if weight == 1:
-                w1_chunks[c] = words[:].rearrange("p (g n) -> p g n", g=D_GROUPS)
+            loads.append(words)
+            if weight == 1 and g is None:
+                w1_words = words[:].rearrange("p (g n) -> p g n", g=D_GROUPS)
                 cols = slice(c * CHUNK_GROUPS * GROUP, (c + 1) * CHUNK_GROUPS * GROUP)
                 nc.sync.dma_start(
-                    out=w1_chunks[c].bitcast(I32),
+                    out=w1_words.bitcast(I32),
                     in_=w1_dram[:, :, cols].rearrange("g p n -> p g n"),
                 )
+                for j in range(CHUNK_GROUPS):
+                    for d in range(D_GROUPS):
+                        w1_groups[CHUNK_GROUPS * c + j, d] = w1_words[:, d, j * BANK : (j + 1) * BANK]
+            elif weight == 1:
+                cols = slice(c * CHUNK_WORDS, (c + 1) * CHUNK_WORDS)
+                nc.sync.dma_start(out=words[:].bitcast(I32), in_=w1_dram[g, :, cols])
+                for j in range(2 * CHUNK_GROUPS):
+                    w1_groups[2 * CHUNK_GROUPS * c + j, g] = words[:, j * BANK : (j + 1) * BANK]
             else:
                 w2_chunks[c] = words[:].rearrange("p (g n) -> p g n", g=CHUNK_GROUPS)
                 pieces = [(0, CHUNK_GROUPS, 0, D)]
@@ -132,6 +146,14 @@ def tile_ffnn_encoder_pc_k_kernel(
 
         for i in range(CHUNK_BUFS):
             load_chunk()
+
+        def last_read(load):
+            weight, c, g = load
+            if weight == 2:
+                return ROUNDS_IN_CHUNK * (c + 1) - 1 + LAG
+            return ROUNDS_IN_CHUNK * (c + 1 if g is None else 2 * (c + 1)) - 1
+
+        freed = 0
 
         h_pairs = h_sb[:].bitcast(F32)
         h_flip = flipped.tile([P, D_GROUPS * 2, P], F32, name="flip")
@@ -194,9 +216,7 @@ def tile_ffnn_encoder_pc_k_kernel(
         sorted_sums = {}
 
         def project(r):
-            w1_words = w1_chunks[r // ROUNDS_IN_CHUNK]
             for G in range(ROUND * r, ROUND * (r + 1)):
-                cols = slice((G % CHUNK_GROUPS) * BANK, (G % CHUNK_GROUPS + 1) * BANK)
                 offset = PACK * (G // 8)
                 plane_cols = slice((G % 8) * BANK, (G % 8 + 1) * BANK)
                 acc = sums.tile([P, BANK], F32, name="acc")
@@ -205,7 +225,7 @@ def tile_ffnn_encoder_pc_k_kernel(
                         out=acc[:],
                         lhsT=h_words[:, g, :].bitcast(FP8X4),
                         lhsT_scale=h_planes[:, g, :],
-                        rhs=w1_words[:, g, cols].bitcast(FP8X4),
+                        rhs=w1_groups[G, g].bitcast(FP8X4),
                         rhs_scale=w1_planes[offset:P, g, plane_cols],
                         start=(g == 0),
                         stop=(g == D_GROUPS - 1),
@@ -260,16 +280,14 @@ def tile_ffnn_encoder_pc_k_kernel(
                 for b in range(D_BANKS):
                     contract_bank(G, b)
 
-        last_in_chunk = ROUNDS_IN_CHUNK - 1
         for i in range(ROUNDS + LAG - ROUNDS_IN_CHUNK):
             if i < ROUNDS:
                 project(i)
-                if i % ROUNDS_IN_CHUNK == last_in_chunk:
-                    load_chunk()
             if i >= LAG:
                 contract(i - LAG)
-                if (i - LAG) % ROUNDS_IN_CHUNK == last_in_chunk:
-                    load_chunk()
+            while last_read(stream[freed]) <= i:
+                freed += 1
+                load_chunk()
             if 1 <= i <= ROUNDS:
                 flip(i - 1)
             if i == SPREAD_STEP:

@@ -20,6 +20,7 @@ EPS = 1e-3
 D_GROUPS = D // GROUP
 F_GROUPS = F // GROUP
 D_BANKS = D // BANK
+HALF = BANK // 2
 QUADS = 4
 SHARED = 4
 
@@ -136,7 +137,8 @@ def tile_ffnn_encoder_pc_k_kernel(
                 w2_chunks[c] = words[:].rearrange("p (g n) -> p g n", g=CHUNK_GROUPS)
                 pieces = [(0, CHUNK_GROUPS, 0, D)]
                 if c == CHUNKS - 1:
-                    pieces = [(0, CHUNK_GROUPS, 0, BANK), (0, ROUND, BANK, D), (ROUND, CHUNK_GROUPS, BANK, D)]
+                    last = CHUNK_GROUPS - 1
+                    pieces = [(0, CHUNK_GROUPS, 0, BANK), (0, last, BANK, D), (last, CHUNK_GROUPS, BANK, D)]
                 for j0, j1, n0, n1 in pieces:
                     groups = slice(CHUNK_GROUPS * c + j0, CHUNK_GROUPS * c + j1)
                     nc.sync.dma_start(
@@ -293,34 +295,41 @@ def tile_ffnn_encoder_pc_k_kernel(
             if i == SPREAD_STEP:
                 spread_vectors()
 
+        halves = [slice(j * HALF, (j + 1) * HALF) for j in range(D // HALF)]
         r_sb = keep.tile([P, D], F32)
-        stats = keep.tile([P, D_BANKS, 6], F32)
+        stats = keep.tile([P, D // HALF, 6], F32)
         for b in range(D_BANKS):
-            cols = slice(b * BANK, (b + 1) * BANK)
             for G in range(F_GROUPS - CHUNK_GROUPS, F_GROUPS):
                 contract_bank(G, b)
-            nc.vector.tensor_tensor(
-                out=r_sb[:, cols], in0=ffn[b][:], in1=resid[:, cols], op=ALU.add
-            )
-            nc.vector.bn_stats(out=stats[:, b, :], in_=r_sb[:, cols])
+            for j in (2 * b, 2 * b + 1):
+                nc.vector.tensor_tensor(
+                    out=r_sb[:, halves[j]],
+                    in0=ffn[b][:, halves[j % 2]],
+                    in1=resid[:, halves[j]],
+                    op=ALU.add,
+                )
+            for j in (2 * b, 2 * b + 1):
+                nc.vector.bn_stats(out=stats[:, j, :], in_=r_sb[:, halves[j]])
         mean_var = keep.tile([P, 2], F32)
         nc.vector.bn_aggr(out=mean_var[:], in_=stats[:].rearrange("p b s -> p (b s)"))
         std = keep.tile([P, 1], F32)
         nc.scalar.activation(out=std[:], in_=mean_var[:, 1:2], func=ACT.Sqrt, bias=eps[:])
         centred = keep.tile([P, D], F32)
-        nc.vector.scalar_tensor_tensor(
-            out=centred[:],
-            in0=r_sb[:],
-            scalar=mean_var[:, 0:1],
-            in1=gain[:],
-            op0=ALU.subtract,
-            op1=ALU.mult,
-        )
         inv_std = keep.tile([P, 1], F32)
-        nc.vector.reciprocal(out=inv_std[:], in_=std[:])
-        normed = keep.tile([P, D], F32)
         for b in range(D_BANKS):
             cols = slice(b * BANK, (b + 1) * BANK)
+            nc.vector.scalar_tensor_tensor(
+                out=centred[:, cols],
+                in0=r_sb[:, cols],
+                scalar=mean_var[:, 0:1],
+                in1=gain[:, cols],
+                op0=ALU.subtract,
+                op1=ALU.mult,
+            )
+            if b == 0:
+                nc.vector.reciprocal(out=inv_std[:], in_=std[:])
+        normed = keep.tile([P, D], F32)
+        for cols in (slice(0, BANK), halves[2], halves[3]):
             nc.vector.scalar_tensor_tensor(
                 out=normed[:, cols],
                 in0=centred[:, cols],

@@ -92,11 +92,12 @@ def tile_ffnn_encoder_pc_k_kernel(
                     in_=s1_dram[g, 4 * q : 4 * q + 4, :].rearrange("r (o n) -> o r n", o=SHARED),
                 )
 
-        for c in range(F_GROUPS // SHARED):
+        s2_by_offset = s2_dram.rearrange("(c o) r n -> o r c n", o=SHARED)
+        for r in range(4):
             for q in range(QUADS):
                 nc.gpsimd.dma_start(
-                    out=w2_planes[32 * q : 32 * q + 16, c, :].bitcast(F32),
-                    in_=s2_dram[SHARED * c : SHARED * (c + 1), 4 * q : 4 * q + 4, :],
+                    out=w2_planes[32 * q + r : 32 * q + 16 : 4, :, :].bitcast(F32),
+                    in_=s2_by_offset[:, 4 * q + r, :, :],
                 )
 
         stream = []

@@ -137,9 +137,16 @@ def tile_ffnn_encoder_pc_k_kernel(
             else:
                 w2_chunks[c] = words[:].rearrange("p (g n) -> p g n", g=CHUNK_GROUPS)
                 pieces = [(0, CHUNK_GROUPS, 0, D)]
+                if c == CHUNKS - 2:
+                    pieces = [(0, ROUND, 0, D), (ROUND, CHUNK_GROUPS, 0, D)]
                 if c == CHUNKS - 1:
                     last = CHUNK_GROUPS - 1
-                    pieces = [(0, CHUNK_GROUPS, 0, BANK), (0, last, BANK, D), (last, CHUNK_GROUPS, BANK, D)]
+                    pieces = [
+                        (0, CHUNK_GROUPS, 0, BANK),
+                        (0, ROUND, BANK, D),
+                        (ROUND, last, BANK, D),
+                        (last, CHUNK_GROUPS, BANK, D),
+                    ]
                 for j0, j1, n0, n1 in pieces:
                     groups = slice(CHUNK_GROUPS * c + j0, CHUNK_GROUPS * c + j1)
                     nc.sync.dma_start(

import concourse.mybir as mybir
from concourse.masks import make_identity

F32 = mybir.dt.float32
BF16 = mybir.dt.bfloat16
I32 = mybir.dt.int32
U32 = mybir.dt.uint32
U8 = mybir.dt.uint8
FP8X4 = mybir.dt.float8_e4m3fn_x4
ALU = mybir.AluOpType
ACT = mybir.ActivationFunctionType

P = 128
PACK = 4
GROUP = P * PACK
BANK = 512
D = 1024
F = 16384
EPS = 1e-3
D_GROUPS = D // GROUP
F_GROUPS = F // GROUP
D_BANKS = D // BANK
HALF = BANK // 2
QUADS = 4
SHARED = 4

CHUNK_GROUPS = 4
CHUNK_WORDS = CHUNK_GROUPS * D
CHUNKS = F_GROUPS // CHUNK_GROUPS
PAIRS = CHUNKS // 2
CHUNK_BUFS = 9
ROUND = 2
ROUNDS = F_GROUPS // ROUND
ROUNDS_IN_CHUNK = CHUNK_GROUPS // ROUND
LEAD = 2
LAG = ROUNDS_IN_CHUNK * LEAD + 1
SPREAD_STEP = 2
STEP_BANKS = 3

FLOPS = 2 * P * D * F * 2


def tile_ffnn_encoder_pc_k_kernel(
    tc, h_attn, W1_words, W1_scales, b1, W2_words, W2_scales, b2, g2, beta2, out
):
    nc = tc.nc
    h_dram = h_attn.flatten_outer_dims()
    out_dram = out.flatten_outer_dims()
    w1_dram = W1_words.rearrange("g p n t -> g p (n t)").bitcast(I32)
    w2_dram = W2_words.rearrange("g p n t -> g p (n t)").bitcast(I32)
    s1_dram = W1_scales.bitcast(F32)
    s2_dram = W2_scales.bitcast(F32)

    with tc.manual_schedule(), tc.tile_pool(name="keep", bufs=1) as keep, tc.tile_pool(
        name="chunks", bufs=CHUNK_BUFS
    ) as chunks, tc.tile_pool(name="work", bufs=2) as work, tc.psum_pool(
        name="sums", bufs=STEP_BANKS
    ) as sums, tc.psum_pool(name="flipped", bufs=STEP_BANKS) as flipped, tc.psum_pool(
        name="total", bufs=1
    ) as total:
        h_sb = keep.tile([P, D], BF16, align_bytes=64)
        nc.scalar.dma_start(out=h_sb[:], in_=h_dram)

        eps = keep.tile([P, 1], F32)
        nc.gpsimd.memset(eps[:], EPS)
        warm = keep.tile([P, 1], F32)
        nc.scalar.activation(out=warm[:], in_=eps[:], func=ACT.Sqrt)
        ident = keep.tile([P, P], F32)
        make_identity(nc, ident[:])

        w1_planes = keep.tile([P, D_GROUPS, F // SHARED], U8, align_bytes=64)
        w2_planes = keep.tile([P, F_GROUPS // SHARED, D], U8, align_bytes=64)
        nc.vector.memset(w1_planes[:].bitcast(I32), 0)
        b1_rows = keep.tile([P, GROUP], BF16)
        nc.vector.memset(b1_rows[:], 0.0)
        vec_rows = keep.tile([P, 3, D], BF16)
        nc.vector.memset(vec_rows[:], 0.0)
        nc.vector.memset(w2_planes[:].bitcast(I32), 0)
        ones = keep.tile([P, P], BF16)
        nc.vector.memset(ones[:], 1.0)

        nc.scalar.dma_start(
            out=b1_rows[0:F_GROUPS, :], in_=b1.rearrange("(g k) -> g k", k=GROUP)
        )
        for i, vec in enumerate((b2, g2, beta2)):
            nc.scalar.dma_start(out=vec_rows[0:1, i, :], in_=vec.rearrange("(o n) -> o n", o=1))

        for g in range(D_GROUPS):
            for q in range(QUADS):
                nc.gpsimd.dma_start(
                    out=w1_planes[32 * q : 32 * q + 16, g, :].bitcast(F32),
                    in_=s1_dram[g, 4 * q : 4 * q + 4, :].rearrange("r (o n) -> o r n", o=SHARED),
                )

        s2_by_offset = s2_dram.rearrange("(c o) r n -> o r c n", o=SHARED)
        for r in range(4):
            for q in range(QUADS):
                nc.gpsimd.dma_start(
                    out=w2_planes[32 * q + r : 32 * q + 16 : 4, :, :].bitcast(F32),
                    in_=s2_by_offset[:, 4 * q + r, :, :],
                )

        stream = []
        for pair in range(PAIRS + 1):
            if pair == 0:
                stream += [(1, 0, None), (1, 1, None)]
            elif pair < PAIRS:
                stream += [(1, pair, g) for g in range(D_GROUPS)]
            if pair >= 1:
                stream += [(2, 2 * pair - 2, None), (2, 2 * pair - 1, None)]
        w1_groups = {}
        w2_chunks = {}
        loads = []

        def load_chunk():
            i = len(loads)
            if i == len(stream):
                return
            weight, c, g = stream[i]
            words = chunks.tile([P, CHUNK_WORDS], U32, name="words", align_bytes=64)
            loads.append(words)
            if weight == 1 and g is None:
                w1_words = words[:].rearrange("p (g n) -> p g n", g=D_GROUPS)
                cols = slice(c * CHUNK_GROUPS * GROUP, (c + 1) * CHUNK_GROUPS * GROUP)
                nc.sync.dma_start(
                    out=w1_words.bitcast(I32),
                    in_=w1_dram[:, :, cols].rearrange("g p n -> p g n"),
                )
                for j in range(CHUNK_GROUPS):
                    for d in range(D_GROUPS):
                        w1_groups[CHUNK_GROUPS * c + j, d] = w1_words[:, d, j * BANK : (j + 1) * BANK]
            elif weight == 1:
                cols = slice(c * CHUNK_WORDS, (c + 1) * CHUNK_WORDS)
                nc.sync.dma_start(out=words[:].bitcast(I32), in_=w1_dram[g, :, cols])
                for j in range(2 * CHUNK_GROUPS):
                    w1_groups[2 * CHUNK_GROUPS * c + j, g] = words[:, j * BANK : (j + 1) * BANK]
            else:
                w2_chunks[c] = words[:].rearrange("p (g n) -> p g n", g=CHUNK_GROUPS)
                pieces = [(0, CHUNK_GROUPS, 0, D)]
                if c == CHUNKS - 2:
                    pieces = [(0, ROUND, 0, D), (ROUND, CHUNK_GROUPS, 0, D)]
                if c == CHUNKS - 1:
                    last = CHUNK_GROUPS - 1
                    pieces = [
                        (0, CHUNK_GROUPS, 0, BANK),
                        (0, ROUND, BANK, D),
                        (ROUND, last, BANK, D),
                        (last, CHUNK_GROUPS, BANK, D),
                    ]
                for j0, j1, n0, n1 in pieces:
                    groups = slice(CHUNK_GROUPS * c + j0, CHUNK_GROUPS * c + j1)
                    nc.sync.dma_start(
                        out=w2_chunks[c][:, j0:j1, n0:n1].bitcast(I32),
                        in_=w2_dram[groups, :, n0:n1].rearrange("g p n -> p g n"),
                    )

        for i in range(CHUNK_BUFS):
            load_chunk()

        def last_read(load):
            weight, c, g = load
            if weight == 2:
                return ROUNDS_IN_CHUNK * (c + 1) - 1 + LAG
            return ROUNDS_IN_CHUNK * (c + 1 if g is None else 2 * (c + 1)) - 1

        freed = 0

        h_pairs = h_sb[:].bitcast(F32)
        h_flip = flipped.tile([P, D_GROUPS * 2, P], F32, name="flip")
        for g in range(D_GROUPS):
            for u in range(2):
                nc.tensor.transpose(
                    h_flip[:, 2 * g + u, :], h_pairs[:, 256 * g + u : 256 * (g + 1) : 2], ident[:]
                )
        h_packed = keep.tile([P, D_GROUPS, P, PACK], BF16, align_bytes=64)
        nc.vector.tensor_copy(
            out=h_packed[:].bitcast(F32), in_=h_flip[:].rearrange("p (g u) m -> p g m u", u=2)
        )
        h_words = keep.tile([P, D_GROUPS, P], U32, align_bytes=64)
        h_planes = keep.tile([P, D_GROUPS, P], U8, align_bytes=64)
        nc.vector.quantize_mx(
            out=h_words[:].rearrange("p g m -> p (g m)").bitcast(FP8X4),
            scales=h_planes[:].rearrange("p g m -> p (g m)"),
            in_=h_packed[:].rearrange("p g m t -> p (g m t)"),
        )

        b1_sorted = keep.tile([P, PACK, P], F32)
        nc.vector.tensor_copy(
            out=b1_sorted[:], in_=b1_rows[:].rearrange("g (p t) -> g t p", t=PACK)
        )
        b1_flip = flipped.tile([P, PACK, P], F32, name="flip")
        for t in range(PACK):
            nc.tensor.transpose(b1_flip[:, t, :], b1_sorted[:, t, :], ident[:])
        b1_t = keep.tile([P, F_GROUPS, PACK], F32)
        nc.vector.tensor_copy(
            out=b1_t[:], in_=b1_flip[:, :, 0:F_GROUPS].rearrange("p t g -> p g t")
        )

        resid = keep.tile([P, D], F32)
        gain = keep.tile([P, D], F32)
        shift = keep.tile([P, D], F32)
        def spread_vectors():
            for b in range(D_BANKS):
                cols = slice(b * BANK, (b + 1) * BANK)
                b2_all = sums.tile([P, BANK], F32, name="acc")
                nc.tensor.matmul(
                    out=b2_all[:], lhsT=ones[:], rhs=vec_rows[:, 0, cols], start=True, stop=True
                )
                nc.vector.tensor_tensor(
                    out=resid[:, cols], in0=b2_all[:], in1=h_sb[:, cols], op=ALU.add
                )
                g2_all = sums.tile([P, BANK], F32, name="acc")
                nc.tensor.matmul(
                    out=g2_all[:], lhsT=ones[:], rhs=vec_rows[:, 1, cols], start=True, stop=True
                )
                nc.scalar.copy(out=gain[:, cols], in_=g2_all[:])
                beta2_all = sums.tile([P, BANK], F32, name="acc")
                nc.tensor.matmul(
                    out=beta2_all[:], lhsT=ones[:], rhs=vec_rows[:, 2, cols], start=True, stop=True
                )
                nc.scalar.copy(out=shift[:, cols], in_=beta2_all[:])

        hid_words = keep.tile([P, F_GROUPS, P], U32, align_bytes=64)
        hid_planes = keep.tile([P, F_GROUPS, P], U8, align_bytes=64)
        ffn = [total.tile([P, BANK], F32, name="ffn%d" % b) for b in range(D_BANKS)]
        sorted_sums = {}

        def project(r):
            for G in range(ROUND * r, ROUND * (r + 1)):
                offset = PACK * (G // 8)
                plane_cols = slice((G % 8) * BANK, (G % 8 + 1) * BANK)
                acc = sums.tile([P, BANK], F32, name="acc")
                for g in range(D_GROUPS):
                    nc.tensor.matmul_mx(
                        out=acc[:],
                        lhsT=h_words[:, g, :].bitcast(FP8X4),
                        lhsT_scale=h_planes[:, g, :],
                        rhs=w1_groups[G, g].bitcast(FP8X4),
                        rhs_scale=w1_planes[offset:P, g, plane_cols],
                        start=(g == 0),
                        stop=(g == D_GROUPS - 1),
                    )
                tidy = work.tile([P, PACK, P], F32, name="tidy", bufs=2 * ROUND)
                nc.scalar.copy(out=tidy[:], in_=acc[:].rearrange("m (p t) -> m t p", t=PACK))
                sorted_sums[G] = tidy

        def flip(r):
            groups = range(ROUND * r, ROUND * (r + 1))
            banks = {}
            for G in groups:
                banks[G] = flipped.tile([P, PACK, P], F32, name="flip")
                for t in range(PACK):
                    nc.tensor.transpose(banks[G][:, t, :], sorted_sums[G][:, t, :], ident[:])
            biased = work.tile([P, ROUND, P, PACK], BF16, name="biased")
            rectified = work.tile([P, ROUND, P * PACK], BF16, name="rectified", align_bytes=64)
            for G in groups:
                nc.vector.tensor_tensor(
                    out=biased[:, G % ROUND, :, :],
                    in0=banks[G][:].rearrange("p t m -> p m t"),
                    in1=b1_t[:, G, :].unsqueeze(1).to_broadcast([P, P, PACK]),
                    op=ALU.add,
                )
            for G in groups:
                nc.vector.tensor_scalar_max(
                    out=rectified[:, G % ROUND, :],
                    in0=biased[:, G % ROUND, :, :].rearrange("p m t -> p (m t)"),
                    scalar1=0.0,
                )
            for G in groups:
                nc.vector.quantize_mx(
                    out=hid_words[:, G, :].bitcast(FP8X4),
                    scales=hid_planes[:, G, :],
                    in_=rectified[:, G % ROUND, :],
                )

        def contract_bank(G, b):
            cols = slice(b * BANK, (b + 1) * BANK)
            nc.tensor.matmul_mx(
                out=ffn[b][:],
                lhsT=hid_words[:, G, :].bitcast(FP8X4),
                lhsT_scale=hid_planes[:, G, :],
                rhs=w2_chunks[G // CHUNK_GROUPS][:, G % CHUNK_GROUPS, cols].bitcast(FP8X4),
                rhs_scale=w2_planes[PACK * (G % SHARED) : P, G // SHARED, cols],
                start=(G == 0),
                stop=(G == F_GROUPS - 1),
            )

        def contract(r):
            for G in range(ROUND * r, ROUND * (r + 1)):
                for b in range(D_BANKS):
                    contract_bank(G, b)

        for i in range(ROUNDS + LAG - ROUNDS_IN_CHUNK):
            if i < ROUNDS:
                project(i)
            if i >= LAG:
                contract(i - LAG)
            while last_read(stream[freed]) <= i:
                freed += 1
                load_chunk()
            if 1 <= i <= ROUNDS:
                flip(i - 1)
            if i == SPREAD_STEP:
                spread_vectors()

        halves = [slice(j * HALF, (j + 1) * HALF) for j in range(D // HALF)]
        r_sb = keep.tile([P, D], F32)
        stats = keep.tile([P, D // HALF, 6], F32)
        for b in range(D_BANKS):
            for G in range(F_GROUPS - CHUNK_GROUPS, F_GROUPS):
                contract_bank(G, b)
            for j in (2 * b, 2 * b + 1):
                nc.vector.tensor_tensor(
                    out=r_sb[:, halves[j]],
                    in0=ffn[b][:, halves[j % 2]],
                    in1=resid[:, halves[j]],
                    op=ALU.add,
                )
            for j in (2 * b, 2 * b + 1):
                nc.vector.bn_stats(out=stats[:, j, :], in_=r_sb[:, halves[j]])
        mean_var = keep.tile([P, 2], F32)
        nc.vector.bn_aggr(out=mean_var[:], in_=stats[:].rearrange("p b s -> p (b s)"))
        std = keep.tile([P, 1], F32)
        nc.scalar.activation(out=std[:], in_=mean_var[:, 1:2], func=ACT.Sqrt, bias=eps[:])
        centred = keep.tile([P, D], F32)
        inv_std = keep.tile([P, 1], F32)
        for b in range(D_BANKS):
            cols = slice(b * BANK, (b + 1) * BANK)
            nc.vector.scalar_tensor_tensor(
                out=centred[:, cols],
                in0=r_sb[:, cols],
                scalar=mean_var[:, 0:1],
                in1=gain[:, cols],
                op0=ALU.subtract,
                op1=ALU.mult,
            )
            if b == 0:
                nc.vector.reciprocal(out=inv_std[:], in_=std[:])
        normed = keep.tile([P, D], F32)
        for cols in (slice(0, BANK), halves[2], halves[3]):
            nc.vector.scalar_tensor_tensor(
                out=normed[:, cols],
                in0=centred[:, cols],
                scalar=inv_std[:],
                in1=shift[:, cols],
                op0=ALU.mult,
                op1=ALU.add,
            )
            nc.sync.dma_start(out=out_dram[:, cols], in_=normed[:, cols])
